import numpy as np
import ml_dtypes


def mxq(x, axis, fmt="e4m3"):
    dtype, down = {"e4m3": (ml_dtypes.float8_e4m3fn, 7), "e5m2": (ml_dtypes.float8_e5m2, 14)}[fmt]
    v = np.moveaxis(np.asarray(x, np.float32).astype(ml_dtypes.bfloat16).astype(np.float64), axis, -1)
    blocks = v.reshape(v.shape[:-1] + (-1, 32))
    amax = np.abs(blocks).max(-1, keepdims=True)
    byte = np.maximum(np.where(amax > 0, np.frexp(amax)[1] - 1 + 127, 0) - down, 1)
    scale = np.exp2(byte - 127.0)
    codes = (blocks / scale).astype(np.float32).astype(dtype).astype(np.float64)
    return np.moveaxis((codes * scale).reshape(v.shape), -1, axis)


WIDE = False


def mx_kscale(k):
    if not WIDE:
        return np.ones(k)
    levels = np.array([10, -10, 5, -5, 0])
    a = np.random.permutation(np.resize(levels, k // 512 * 4)).reshape(k // 512, 4)
    idx = np.arange(k)
    return np.exp2(a[idx // 512, idx % 128 // 32])


BF16 = ml_dtypes.bfloat16


def bf(x):
    return np.asarray(x, np.float32).astype(BF16)


def f64(x):
    return np.asarray(x).astype(np.float64)


B, G, FI, FO, H, W = 1, 8, 8192, 128, 8, 16
ITERS = 3


def sigmoid(v):
    return 1.0 / (1.0 + np.exp(-v))


def setup_inputs():
    s = mx_kscale(FI)
    gain = 0.5 + np.random.random((B, G, 1, H, W))
    x = np.random.standard_normal((B, G, FI, H, W)) * gain * s[:, None, None]
    weight = np.random.standard_normal((FO, G, FI)) * np.sqrt(2.0 / (FI * FO)) / s
    bias = np.random.standard_normal((1, FO, 1, 1)) * np.sqrt(2.0 * G / FO)
    return {"x": bf(x.reshape(B, G * FI, H, W)), "weight": bf(weight.reshape(FO, G * FI, 1, 1)), "bias": bf(bias)}


def reference(x, weight, bias):
    w = f64(weight)[:, :, 0, 0].reshape(FO, G, FI).transpose(1, 0, 2)
    xr = f64(x).reshape(B, G, FI, H * W)
    con = (mxq(w, 2, "e4m3")[None] @ mxq(xr, 2, "e4m3")).reshape(B, G, FO, H, W)
    beta = 0.0
    for i in range(ITERS):
        alpha = sigmoid(beta)
        v = np.sum(alpha * con, axis=1, keepdims=True)
        if i == ITERS - 1:
            return v[:, 0] + f64(bias)
        beta = beta + np.sum(v * con, axis=2, keepdims=True)

@@ -1,0 +1,215 @@
+from contextlib import ExitStack
+
+import concourse.mybir as mybir
+from concourse.masks import make_identity
+
+F32 = mybir.dt.float32
+BF16 = mybir.dt.bfloat16
+U32 = mybir.dt.uint32
+U8 = mybir.dt.uint8
+FP8X4 = mybir.dt.float8_e4m3fn_x4
+ADD = mybir.AluOpType.add
+MULT = mybir.AluOpType.mult
+AXIS_X = mybir.AxisListType.X
+SIGMOID = mybir.ActivationFunctionType.Sigmoid
+
+P = 128
+PACK = 4
+K_PASS = P * PACK
+GROUPS = 8
+GROUP_CHANNELS = 8192
+OUT_CHANNELS = 128
+PIXELS = 128
+GROUP_PASSES = GROUP_CHANNELS // K_PASS
+PASSES = GROUPS * GROUP_PASSES
+
+STEP_PASSES = 4
+STEPS = PASSES // STEP_PASSES
+STEP_CHANNELS = STEP_PASSES * K_PASS
+WEIGHT_LOAD_STEPS = 2
+BANK_PASSES = 2
+BANK_GROUPS = 4
+
+FLOPS = 2 * OUT_CHANNELS * GROUPS * GROUP_CHANNELS * PIXELS
+
+
+def tile_dynamicrouting_k_kernel(tc, x, weight, bias, out):
+    nc = tc.nc
+    x_rows = x.rearrange("b c h w -> (b c) (h w)")
+    w_rows = weight.rearrange("o c a b -> o (c a b)")
+    bias_row = bias.rearrange("a o b c -> a (o b c)")
+    out_rows = out.rearrange("b o h w -> (b o) (h w)")
+
+    with ExitStack() as ctx:
+        const = ctx.enter_context(tc.tile_pool(name="const", bufs=1))
+        raw = ctx.enter_context(tc.tile_pool(name="raw", bufs=8))
+        stage = ctx.enter_context(tc.tile_pool(name="stage", bufs=3))
+        routing = ctx.enter_context(tc.tile_pool(name="routing", bufs=1))
+        banks = ctx.enter_context(tc.psum_pool(name="banks", bufs=6))
+        sums = ctx.enter_context(tc.psum_pool(name="sums", bufs=1))
+
+        ctx.enter_context(tc.manual_schedule())
+
+        ident = const.tile([P, P], F32)
+        make_identity(nc, ident[:])
+        beta = routing.tile([P, GROUPS], F32)
+        nc.vector.memset(beta[:], 0.0)
+
+        warm = const.tile([P, 1], F32)
+        nc.vector.memset(warm[:], 0.0)
+        nc.scalar.activation(out=warm[:], in_=warm[:], func=SIGMOID)
+
+        bias_square = const.tile([P, P], BF16)
+        nc.vector.memset(bias_square[:], 0.0)
+        nc.sync.dma_start(out=bias_square[0:1, :], in_=bias_row)
+        bias_square_f32 = const.tile([P, P], F32)
+        nc.vector.tensor_copy(out=bias_square_f32[:], in_=bias_square[:])
+        bias_bank = banks.tile([P, P], F32, tag="bank")
+        nc.tensor.transpose(bias_bank[:], bias_square_f32[:], ident[:])
+        bias_col = const.tile([P, 1], F32)
+        nc.vector.tensor_copy(out=bias_col[:], in_=bias_bank[:, 0:1])
+
+        con_low = sums.tile([P, BANK_GROUPS, OUT_CHANNELS], F32)
+        con_high = sums.tile([P, BANK_GROUPS, OUT_CHANNELS], F32)
+        con_banks = [con_low, con_high]
+
+        w_raw_of = {}
+        w_banks_of = {}
+        w_grouped_of = {}
+        w_quantised_of = {}
+        x_raw_of = {}
+        x_grouped_of = {}
+        x_quantised_of = {}
+
+        def exists(step):
+            return 0 <= step < STEPS
+
+        def load_weight(step):
+            if not exists(step) or step % WEIGHT_LOAD_STEPS != 0:
+                return
+            k0 = step * STEP_CHANNELS
+            w_raw = raw.tile([P, WEIGHT_LOAD_STEPS * STEP_CHANNELS], BF16)
+            nc.sync.dma_start(out=w_raw[:], in_=w_rows[:, k0 : k0 + WEIGHT_LOAD_STEPS * STEP_CHANNELS])
+            for s in range(WEIGHT_LOAD_STEPS):
+                w_raw_of[step + s] = w_raw[:, s * STEP_CHANNELS : (s + 1) * STEP_CHANNELS]
+
+        def transpose_weight(step):
+            if not exists(step):
+                return
+            w_words = w_raw_of[step].bitcast(F32).rearrange("o (c p u) -> o c u p", p=P, u=2)
+            w_banks_of[step] = []
+            for c0 in range(0, STEP_PASSES, BANK_PASSES):
+                bank = banks.tile([P, BANK_PASSES, 2, OUT_CHANNELS], F32, tag="bank")
+                for c in range(BANK_PASSES):
+                    for u in range(2):
+                        nc.tensor.transpose(bank[:, c, u, :], w_words[:, c0 + c, u, :], ident[:])
+                w_banks_of[step].append(bank)
+
+        def copy_weight_out(step):
+            if not exists(step):
+                return
+            w_grouped = stage.tile([P, STEP_PASSES * OUT_CHANNELS * PACK], BF16, align_bytes=64)
+            w_grouped_words = w_grouped[:].bitcast(F32).rearrange("p (b c o u) -> p b c o u", c=BANK_PASSES, o=OUT_CHANNELS, u=2)
+            for b, bank in enumerate(w_banks_of[step]):
+                nc.scalar.copy(out=w_grouped_words[:, b], in_=bank[:].rearrange("p c u o -> p c o u"))
+            w_grouped_of[step] = w_grouped
+
+        def quantise_weight(step):
+            if not exists(step):
+                return
+            w_codes = stage.tile([P, STEP_PASSES * OUT_CHANNELS], U32, align_bytes=64, bufs=5)
+            w_scales = stage.tile([P, STEP_PASSES * OUT_CHANNELS], U8, align_bytes=64, bufs=5)
+            nc.vector.quantize_mx(out=w_codes[:].bitcast(FP8X4), scales=w_scales[:], in_=w_grouped_of[step][:])
+            w_quantised_of[step] = (w_codes, w_scales)
+
+        def load_x(step):
+            if not exists(step):
+                return
+            k0 = step * STEP_CHANNELS
+            x_raw = raw.tile([P, STEP_PASSES, PACK, PIXELS], BF16, bufs=12)
+            nc.sync.dma_start(
+                out=x_raw[:],
+                in_=x_rows[k0 : k0 + STEP_CHANNELS, :].rearrange("(c p t) n -> p c t n", p=P, t=PACK),
+            )
+            x_raw_of[step] = x_raw
+
+        def regroup_x(step):
+            if not exists(step):
+                return
+            vector_passes = STEP_PASSES - 1 - step % 2
+            x_grouped = stage.tile([P, STEP_PASSES, PIXELS, PACK], BF16, align_bytes=64)
+            x_from = x_raw_of[step][:].rearrange("p c t (m i) -> p c m t i", i=4)
+            x_to = x_grouped[:].rearrange("p c (m i) t -> p c m t i", i=4)
+            nc.vector.tensor_copy(out=x_to[:, :vector_passes], in_=x_from[:, :vector_passes])
+            for c in range(vector_passes, STEP_PASSES):
+                nc.scalar.copy(out=x_to[:, c], in_=x_from[:, c])
+            x_grouped_of[step] = x_grouped
+
+        def quantise_x(step):
+            if not exists(step):
+                return
+            x_codes = stage.tile([P, STEP_PASSES * PIXELS], U32, align_bytes=64)
+            x_scales = stage.tile([P, STEP_PASSES * PIXELS], U8, align_bytes=64)
+            nc.vector.quantize_mx(
+                out=x_codes[:].bitcast(FP8X4),
+                scales=x_scales[:],
+                in_=x_grouped_of[step][:].rearrange("p c n t -> p (c n t)"),
+            )
+            x_quantised_of[step] = (x_codes, x_scales)
+
+        def multiply(step):
+            if not exists(step):
+                return
+            w_codes, w_scales = w_quantised_of[step]
+            x_codes, x_scales = x_quantised_of[step]
+            for c in range(STEP_PASSES):
+                g, c_in_group = divmod(step * STEP_PASSES + c, GROUP_PASSES)
+                cols = slice(c * P, (c + 1) * P)
+                nc.tensor.matmul_mx(
+                    out=con_banks[g // BANK_GROUPS][:, g % BANK_GROUPS, :],
+                    lhsT=x_codes[:, cols].bitcast(FP8X4),
+                    lhsT_scale=x_scales[:, cols],
+                    rhs=w_codes[:, cols].bitcast(FP8X4),
+                    rhs_scale=w_scales[:, cols],
+                    start=(c_in_group == 0),
+                    stop=(c_in_group == GROUP_PASSES - 1),
+                )
+
+        for t in range(-4, STEPS + 1):
+            load_weight(t + 4)
+            load_x(t)
+            regroup_x(t)
+            multiply(t - 1)
+            copy_weight_out(t + 3)
+            transpose_weight(t + 4)
+            quantise_weight(t + 2)
+            quantise_x(t)
+
+        def times_con(factor_of_bank):
+            product = routing.tile([P, GROUPS, OUT_CHANNELS], F32, tag="product")
+            for b in range(GROUPS // BANK_GROUPS):
+                nc.vector.tensor_tensor(
+                    out=product[:, b * BANK_GROUPS : (b + 1) * BANK_GROUPS, :],
+                    in0=con_banks[b][:],
+                    in1=factor_of_bank(b).to_broadcast([P, BANK_GROUPS, OUT_CHANNELS]),
+                    op=MULT,
+                )
+            return product
+
+        for round_index in range(3):
+            alpha = routing.tile([P, GROUPS], F32, tag="alpha")
+            nc.scalar.activation(out=alpha[:], in_=beta[:], func=SIGMOID)
+            weighted = times_con(lambda b: alpha[:, b * BANK_GROUPS : (b + 1) * BANK_GROUPS].unsqueeze(2))
+            v = routing.tile([P, OUT_CHANNELS], F32, tag="v")
+            nc.vector.tensor_reduce(out=v[:], in_=weighted[:].rearrange("p g o -> p o g"), axis=AXIS_X, op=ADD)
+            if round_index < 2:
+                agreeing = times_con(lambda b: v[:].unsqueeze(1))
+                agreement = routing.tile([P, GROUPS], F32, tag="agreement")
+                nc.vector.tensor_reduce(out=agreement[:], in_=agreeing[:], axis=AXIS_X, op=ADD)
+                nc.vector.tensor_tensor(out=beta[:], in0=beta[:], in1=agreement[:], op=ADD)
+
+        v_bank = banks.tile([P, P], F32, tag="bank")
+        nc.tensor.transpose(v_bank[:], v[:], ident[:])
+        result = routing.tile([P, PIXELS], F32)
+        nc.vector.tensor_scalar(out=result[:], in0=v_bank[:], scalar1=bias_col[:, 0:1], scalar2=None, op0=ADD)
+        nc.sync.dma_start(out=out_rows, in_=result[:])

@@ -12,6 +12,8 @@ ADD = mybir.AluOpType.add
 MULT = mybir.AluOpType.mult
 AXIS_X = mybir.AxisListType.X
 SIGMOID = mybir.ActivationFunctionType.Sigmoid
+SQUARE = mybir.ActivationFunctionType.Square
+COPY = mybir.ActivationFunctionType.Copy
 
 P = 128
 PACK = 4
@@ -25,10 +27,13 @@ PASSES = GROUPS * GROUP_PASSES
 
 STEP_PASSES = 4
 STEPS = PASSES // STEP_PASSES
+GROUP_STEPS = GROUP_PASSES // STEP_PASSES
 STEP_CHANNELS = STEP_PASSES * K_PASS
 WEIGHT_LOAD_STEPS = 2
 BANK_PASSES = 2
-BANK_GROUPS = 4
+BANK_WORDS = 512
+ROUND_DOTS = 2
+SUMMED_ON_VECTOR = 4
 
 FLOPS = 2 * OUT_CHANNELS * GROUPS * GROUP_CHANNELS * PIXELS
 
@@ -46,14 +51,12 @@ def tile_dynamicrouting_k_kernel(tc, x, weight, bias, out):
         stage = ctx.enter_context(tc.tile_pool(name="stage", bufs=3))
         routing = ctx.enter_context(tc.tile_pool(name="routing", bufs=1))
         banks = ctx.enter_context(tc.psum_pool(name="banks", bufs=6))
-        sums = ctx.enter_context(tc.psum_pool(name="sums", bufs=1))
+        sums = ctx.enter_context(tc.psum_pool(name="sums", bufs=2))
 
         ctx.enter_context(tc.manual_schedule())
 
         ident = const.tile([P, P], F32)
         make_identity(nc, ident[:])
-        beta = routing.tile([P, GROUPS], F32)
-        nc.vector.memset(beta[:], 0.0)
 
         warm = const.tile([P, 1], F32)
         nc.vector.memset(warm[:], 0.0)
@@ -61,17 +64,16 @@ def tile_dynamicrouting_k_kernel(tc, x, weight, bias, out):
 
         bias_square = const.tile([P, P], BF16)
         nc.vector.memset(bias_square[:], 0.0)
-        nc.sync.dma_start(out=bias_square[0:1, :], in_=bias_row)
+        nc.scalar.dma_start(out=bias_square[0:1, :], in_=bias_row)
         bias_square_f32 = const.tile([P, P], F32)
-        nc.vector.tensor_copy(out=bias_square_f32[:], in_=bias_square[:])
-        bias_bank = banks.tile([P, P], F32, tag="bank")
-        nc.tensor.transpose(bias_bank[:], bias_square_f32[:], ident[:])
-        bias_col = const.tile([P, 1], F32)
-        nc.vector.tensor_copy(out=bias_col[:], in_=bias_bank[:, 0:1])
+        ones = const.tile([P, P], F32)
+        nc.vector.memset(ones[:], 1.0)
 
-        con_low = sums.tile([P, BANK_GROUPS, OUT_CHANNELS], F32)
-        con_high = sums.tile([P, BANK_GROUPS, OUT_CHANNELS], F32)
-        con_banks = [con_low, con_high]
+        con = routing.tile([P, GROUPS, OUT_CHANNELS], F32)
+        gram = routing.tile([P, GROUPS, GROUPS], F32)
+        vector_scratch = routing.tile([P, OUT_CHANNELS], F32)
+        scalar_scratch = routing.tile([P, OUT_CHANNELS], F32)
+        con_bank_of = {}
 
         w_raw_of = {}
         w_banks_of = {}
@@ -140,7 +142,9 @@ def tile_dynamicrouting_k_kernel(tc, x, weight, bias, out):
             x_grouped = stage.tile([P, STEP_PASSES, PIXELS, PACK], BF16, align_bytes=64)
             x_from = x_raw_of[step][:].rearrange("p c t (m i) -> p c m t i", i=4)
             x_to = x_grouped[:].rearrange("p c (m i) t -> p c m t i", i=4)
-            nc.vector.tensor_copy(out=x_to[:, :vector_passes], in_=x_from[:, :vector_passes])
+            nc.vector.tensor_copy(out=x_to[:, :2], in_=x_from[:, :2])
+            for c in range(2, vector_passes):
+                nc.vector.tensor_copy(out=x_to[:, c], in_=x_from[:, c])
             for c in range(vector_passes, STEP_PASSES):
                 nc.scalar.copy(out=x_to[:, c], in_=x_from[:, c])
             x_grouped_of[step] = x_grouped
@@ -164,9 +168,12 @@ def tile_dynamicrouting_k_kernel(tc, x, weight, bias, out):
             x_codes, x_scales = x_quantised_of[step]
             for c in range(STEP_PASSES):
                 g, c_in_group = divmod(step * STEP_PASSES + c, GROUP_PASSES)
+                if c_in_group == 0:
+                    con_bank = sums.tile([P, BANK_WORDS], F32)
+                    con_bank_of[g] = con_bank
                 cols = slice(c * P, (c + 1) * P)
                 nc.tensor.matmul_mx(
-                    out=con_banks[g // BANK_GROUPS][:, g % BANK_GROUPS, :],
+                    out=con_bank_of[g][:, :OUT_CHANNELS],
                     lhsT=x_codes[:, cols].bitcast(FP8X4),
                     lhsT_scale=x_scales[:, cols],
                     rhs=w_codes[:, cols].bitcast(FP8X4),
@@ -174,6 +181,20 @@ def tile_dynamicrouting_k_kernel(tc, x, weight, bias, out):
                     start=(c_in_group == 0),
                     stop=(c_in_group == GROUP_PASSES - 1),
                 )
+
+        def take_con(g):
+            nc.scalar.copy(out=con[:, g, :], in_=con_bank_of[g][:, :OUT_CHANNELS])
+            nc.scalar.activation(out=scalar_scratch[:], in_=con[:, g, :], func=SQUARE, accum_out=gram[:, g, g : g + 1])
+
+        def dot(g, h):
+            nc.vector.scalar_tensor_tensor(
+                out=vector_scratch[:], in0=con[:, g, :], scalar=1.0, in1=con[:, h, :], op0=MULT, op1=MULT, accum_out=gram[:, g, h : h + 1]
+            )
+
+        def mirror(g):
+            nc.scalar.copy(out=gram[:, 0:g, g], in_=gram[:, g, 0:g])
+
+        dots_to_do = []
 
         for t in range(-4, STEPS + 1):
             load_weight(t + 4)
@@ -183,33 +204,65 @@ def tile_dynamicrouting_k_kernel(tc, x, weight, bias, out):
             copy_weight_out(t + 3)
             transpose_weight(t + 4)
             quantise_weight(t + 2)
+            for _ in range(min(ROUND_DOTS, len(dots_to_do))):
+                g, h = dots_to_do.pop(0)
+                dot(g, h)
+                if h == g - 1:
+                    mirror(g)
             quantise_x(t)
+            if t == 2:
+                nc.vector.tensor_copy(out=bias_square_f32[:], in_=bias_square[:])
+            group, step_in_group = divmod(t, GROUP_STEPS)
+            if t > 0 and step_in_group == 0:
+                take_con(group - 1)
+                dots_to_do.extend((group - 1, h) for h in range(group - 1))
 
-        def times_con(factor_of_bank):
-            product = routing.tile([P, GROUPS, OUT_CHANNELS], F32, tag="product")
-            for b in range(GROUPS // BANK_GROUPS):
-                nc.vector.tensor_tensor(
-                    out=product[:, b * BANK_GROUPS : (b + 1) * BANK_GROUPS, :],
-                    in0=con_banks[b][:],
-                    in1=factor_of_bank(b).to_broadcast([P, BANK_GROUPS, OUT_CHANNELS]),
-                    op=MULT,
+        last = GROUPS - 1
+        early_sum = routing.tile([P, GROUPS], F32)
+        nc.vector.tensor_reduce(out=early_sum[:, :last], in_=gram[:, :last, :last], axis=AXIS_X, op=ADD)
+        for g, h in dots_to_do:
+            dot(g, h)
+        mirror(last)
+
+        row_sum = routing.tile([P, GROUPS], F32)
+        nc.vector.tensor_tensor(out=row_sum[:, :last], in0=early_sum[:, :last], in1=gram[:, last, :last], op=ADD)
+        nc.vector.tensor_reduce(out=row_sum[:, last:], in_=gram[:, last, :], axis=AXIS_X, op=ADD)
+        alpha = routing.tile([P, GROUPS], F32)
+        nc.scalar.activation(out=alpha[:], in_=row_sum[:], func=SIGMOID, scale=0.5)
+
+        terms = routing.tile([P, GROUPS, GROUPS + 1], F32)
+        nc.vector.tensor_scalar(out=terms[:, :, GROUPS], in0=row_sum[:], scalar1=0.5, scalar2=None, op0=MULT)
+        nc.vector.tensor_tensor(
+            out=terms[:, :, :GROUPS], in0=gram[:], in1=alpha[:].unsqueeze(1).to_broadcast([P, GROUPS, GROUPS]), op=MULT
+        )
+        beta = routing.tile([P, GROUPS], F32)
+        nc.vector.tensor_reduce(out=beta[:], in_=terms[:], axis=AXIS_X, op=ADD)
+        last_alpha = routing.tile([P, GROUPS], F32)
+        nc.scalar.activation(out=last_alpha[:], in_=beta[:], func=SIGMOID)
+
+        out_bank = banks.tile([P, BANK_WORDS], F32, tag="bank")
+        nc.tensor.matmul(out_bank[:, :PIXELS], lhsT=bias_square_f32[:], rhs=ones[:], start=True, stop=False)
+        even_odd = routing.tile([P, 2, OUT_CHANNELS], F32)
+        for g in range(SUMMED_ON_VECTOR):
+            if g < 2:
+                nc.vector.tensor_scalar(
+                    out=even_odd[:, g, :], in0=con[:, g, :], scalar1=last_alpha[:, g : g + 1], scalar2=None, op0=MULT
                 )
-            return product
-
-        for round_index in range(3):
-            alpha = routing.tile([P, GROUPS], F32, tag="alpha")
-            nc.scalar.activation(out=alpha[:], in_=beta[:], func=SIGMOID)
-            weighted = times_con(lambda b: alpha[:, b * BANK_GROUPS : (b + 1) * BANK_GROUPS].unsqueeze(2))
-            v = routing.tile([P, OUT_CHANNELS], F32, tag="v")
-            nc.vector.tensor_reduce(out=v[:], in_=weighted[:].rearrange("p g o -> p o g"), axis=AXIS_X, op=ADD)
-            if round_index < 2:
-                agreeing = times_con(lambda b: v[:].unsqueeze(1))
-                agreement = routing.tile([P, GROUPS], F32, tag="agreement")
-                nc.vector.tensor_reduce(out=agreement[:], in_=agreeing[:], axis=AXIS_X, op=ADD)
-                nc.vector.tensor_tensor(out=beta[:], in0=beta[:], in1=agreement[:], op=ADD)
-
-        v_bank = banks.tile([P, P], F32, tag="bank")
-        nc.tensor.transpose(v_bank[:], v[:], ident[:])
+            else:
+                nc.vector.scalar_tensor_tensor(
+                    out=even_odd[:, g % 2, :],
+                    in0=con[:, g, :],
+                    scalar=last_alpha[:, g : g + 1],
+                    in1=even_odd[:, g % 2, :],
+                    op0=MULT,
+                    op1=ADD,
+                )
+        diagonals = routing.tile([P, GROUPS - SUMMED_ON_VECTOR, PIXELS], F32)
+        for d, g in enumerate(range(SUMMED_ON_VECTOR, GROUPS)):
+            nc.scalar.activation(out=diagonals[:, d, :], in_=ident[:], func=COPY, scale=last_alpha[:, g : g + 1])
+            nc.tensor.matmul(out_bank[:, :PIXELS], lhsT=con[:, g, :], rhs=diagonals[:, d, :], start=False, stop=False)
+        for e in range(2):
+            nc.tensor.matmul(out_bank[:, :PIXELS], lhsT=even_odd[:, e, :], rhs=ident[:], start=False, stop=(e == 1))
         result = routing.tile([P, PIXELS], F32)
-        nc.vector.tensor_scalar(out=result[:], in0=v_bank[:], scalar1=bias_col[:, 0:1], scalar2=None, op0=ADD)
+        nc.vector.tensor_copy(out=result[:], in_=out_bank[:, :PIXELS])
         nc.sync.dma_start(out=out_rows, in_=result[:])

@@ -32,7 +32,10 @@ STEP_CHANNELS = STEP_PASSES * K_PASS
 WEIGHT_LOAD_STEPS = 2
 BANK_PASSES = 2
 BANK_WORDS = 512
-ROUND_DOTS = 2
+WARMING_PASSES = 2
+TAKE_ROUND = 5
+MIRROR_ROUND = 10
+ROUND_DOTS = 3
 SUMMED_ON_VECTOR = 4
 
 FLOPS = 2 * OUT_CHANNELS * GROUPS * GROUP_CHANNELS * PIXELS
@@ -50,7 +53,8 @@ def tile_dynamicrouting_k_kernel(tc, x, weight, bias, out):
         raw = ctx.enter_context(tc.tile_pool(name="raw", bufs=8))
         stage = ctx.enter_context(tc.tile_pool(name="stage", bufs=3))
         routing = ctx.enter_context(tc.tile_pool(name="routing", bufs=1))
-        banks = ctx.enter_context(tc.psum_pool(name="banks", bufs=6))
+        banks = ctx.enter_context(tc.psum_pool(name="banks", bufs=5))
+        warming = ctx.enter_context(tc.psum_pool(name="warming", bufs=1))
         sums = ctx.enter_context(tc.psum_pool(name="sums", bufs=2))
 
         ctx.enter_context(tc.manual_schedule())
@@ -71,9 +75,10 @@ def tile_dynamicrouting_k_kernel(tc, x, weight, bias, out):
 
         con = routing.tile([P, GROUPS, OUT_CHANNELS], F32)
         gram = routing.tile([P, GROUPS, GROUPS], F32)
-        vector_scratch = routing.tile([P, OUT_CHANNELS], F32)
+        vector_scratch = routing.tile([P, GROUPS, OUT_CHANNELS], F32)
         scalar_scratch = routing.tile([P, OUT_CHANNELS], F32)
         con_bank_of = {}
+        warm_bank = warming.tile([P, BANK_WORDS], F32)
 
         w_raw_of = {}
         w_banks_of = {}
@@ -182,13 +187,29 @@ def tile_dynamicrouting_k_kernel(tc, x, weight, bias, out):
                     stop=(c_in_group == GROUP_PASSES - 1),
                 )
 
+        def keep_warm(step):
+            if not exists(step):
+                return
+            w_codes, w_scales = w_quantised_of[step]
+            x_codes, x_scales = x_quantised_of[step]
+            for _ in range(WARMING_PASSES):
+                nc.tensor.matmul_mx(
+                    out=warm_bank[:],
+                    lhsT=x_codes[:, :PIXELS].bitcast(FP8X4),
+                    lhsT_scale=x_scales[:, :PIXELS],
+                    rhs=w_codes[:].bitcast(FP8X4),
+                    rhs_scale=w_scales[:],
+                    start=True,
+                    stop=True,
+                )
+
         def take_con(g):
             nc.scalar.copy(out=con[:, g, :], in_=con_bank_of[g][:, :OUT_CHANNELS])
             nc.scalar.activation(out=scalar_scratch[:], in_=con[:, g, :], func=SQUARE, accum_out=gram[:, g, g : g + 1])
 
         def dot(g, h):
             nc.vector.scalar_tensor_tensor(
-                out=vector_scratch[:], in0=con[:, g, :], scalar=1.0, in1=con[:, h, :], op0=MULT, op1=MULT, accum_out=gram[:, g, h : h + 1]
+                out=vector_scratch[:, h, :], in0=con[:, g, :], scalar=1.0, in1=con[:, h, :], op0=MULT, op1=MULT, accum_out=gram[:, g, h : h + 1]
             )
 
         def mirror(g):
@@ -201,27 +222,31 @@ def tile_dynamicrouting_k_kernel(tc, x, weight, bias, out):
             load_x(t)
             regroup_x(t)
             multiply(t - 1)
+            keep_warm(t - 1)
             copy_weight_out(t + 3)
             transpose_weight(t + 4)
             quantise_weight(t + 2)
             for _ in range(min(ROUND_DOTS, len(dots_to_do))):
                 g, h = dots_to_do.pop(0)
                 dot(g, h)
-                if h == g - 1:
-                    mirror(g)
             quantise_x(t)
             if t == 2:
                 nc.vector.tensor_copy(out=bias_square_f32[:], in_=bias_square[:])
-            group, step_in_group = divmod(t, GROUP_STEPS)
-            if t > 0 and step_in_group == 0:
-                take_con(group - 1)
-                dots_to_do.extend((group - 1, h) for h in range(group - 1))
+            group, step_in_group = divmod(t - TAKE_ROUND, GROUP_STEPS)
+            if step_in_group == 0 and 0 <= group < GROUPS - 1:
+                take_con(group)
+                dots_to_do.extend((group, h) for h in range(group))
+            group, step_in_group = divmod(t - MIRROR_ROUND, GROUP_STEPS)
+            if step_in_group == 0 and 0 < group < GROUPS - 2:
+                mirror(group)
 
         last = GROUPS - 1
+        mirror(last - 1)
+        take_con(last)
         early_sum = routing.tile([P, GROUPS], F32)
         nc.vector.tensor_reduce(out=early_sum[:, :last], in_=gram[:, :last, :last], axis=AXIS_X, op=ADD)
-        for g, h in dots_to_do:
-            dot(g, h)
+        for h in range(last):
+            dot(last, h)
         mirror(last)
 
         row_sum = routing.tile([P, GROUPS], F32)

@@ -32,6 +32,8 @@ STEP_CHANNELS = STEP_PASSES * K_PASS
 WEIGHT_LOAD_STEPS = 2
 BANK_PASSES = 2
 BANK_WORDS = 512
+VECTOR_PASSES = 2
+TAIL_WARMING_PASSES = 10
 WARMING_PASSES = 2
 TAKE_ROUND = 5
 MIRROR_ROUND = 10
@@ -143,15 +145,11 @@ def tile_dynamicrouting_k_kernel(tc, x, weight, bias, out):
         def regroup_x(step):
             if not exists(step):
                 return
-            vector_passes = STEP_PASSES - 1 - step % 2
             x_grouped = stage.tile([P, STEP_PASSES, PIXELS, PACK], BF16, align_bytes=64)
             x_from = x_raw_of[step][:].rearrange("p c t (m i) -> p c m t i", i=4)
             x_to = x_grouped[:].rearrange("p c (m i) t -> p c m t i", i=4)
-            nc.vector.tensor_copy(out=x_to[:, :2], in_=x_from[:, :2])
-            for c in range(2, vector_passes):
-                nc.vector.tensor_copy(out=x_to[:, c], in_=x_from[:, c])
-            for c in range(vector_passes, STEP_PASSES):
-                nc.scalar.copy(out=x_to[:, c], in_=x_from[:, c])
+            nc.vector.tensor_copy(out=x_to[:, :VECTOR_PASSES], in_=x_from[:, :VECTOR_PASSES])
+            nc.scalar.copy(out=x_to[:, VECTOR_PASSES:], in_=x_from[:, VECTOR_PASSES:])
             x_grouped_of[step] = x_grouped
 
         def quantise_x(step):
@@ -187,12 +185,12 @@ def tile_dynamicrouting_k_kernel(tc, x, weight, bias, out):
                     stop=(c_in_group == GROUP_PASSES - 1),
                 )
 
-        def keep_warm(step):
+        def keep_warm(step, passes):
             if not exists(step):
                 return
             w_codes, w_scales = w_quantised_of[step]
             x_codes, x_scales = x_quantised_of[step]
-            for _ in range(WARMING_PASSES):
+            for _ in range(passes):
                 nc.tensor.matmul_mx(
                     out=warm_bank[:],
                     lhsT=x_codes[:, :PIXELS].bitcast(FP8X4),
@@ -222,7 +220,7 @@ def tile_dynamicrouting_k_kernel(tc, x, weight, bias, out):
             load_x(t)
             regroup_x(t)
             multiply(t - 1)
-            keep_warm(t - 1)
+            keep_warm(t - 1, TAIL_WARMING_PASSES if t == STEPS else WARMING_PASSES)
             copy_weight_out(t + 3)
             transpose_weight(t + 4)
             quantise_weight(t + 2)

@@ -32,13 +32,12 @@ STEP_CHANNELS = STEP_PASSES * K_PASS
 WEIGHT_LOAD_STEPS = 2
 BANK_PASSES = 2
 BANK_WORDS = 512
-VECTOR_PASSES = 2
-TAIL_WARMING_PASSES = 10
-WARMING_PASSES = 2
-TAKE_ROUND = 5
-MIRROR_ROUND = 10
+X_FALLS_BACK = 4
+WARMING_PASSES = 10
+TAKE_LAG = 1
+MIRROR_LAG = 5
 ROUND_DOTS = 3
-SUMMED_ON_VECTOR = 4
+SUMMED_ON_VECTOR = 6
 
 FLOPS = 2 * OUT_CHANNELS * GROUPS * GROUP_CHANNELS * PIXELS
 
@@ -93,13 +92,17 @@ def tile_dynamicrouting_k_kernel(tc, x, weight, bias, out):
         def exists(step):
             return 0 <= step < STEPS
 
+        weight_loads = {0: 1, 1: 1}
+        weight_loads.update({step: WEIGHT_LOAD_STEPS for step in range(2, STEPS, WEIGHT_LOAD_STEPS)})
+
         def load_weight(step):
-            if not exists(step) or step % WEIGHT_LOAD_STEPS != 0:
+            if step not in weight_loads:
                 return
             k0 = step * STEP_CHANNELS
+            channels = weight_loads[step] * STEP_CHANNELS
             w_raw = raw.tile([P, WEIGHT_LOAD_STEPS * STEP_CHANNELS], BF16)
-            nc.sync.dma_start(out=w_raw[:], in_=w_rows[:, k0 : k0 + WEIGHT_LOAD_STEPS * STEP_CHANNELS])
-            for s in range(WEIGHT_LOAD_STEPS):
+            nc.sync.dma_start(out=w_raw[:, :channels], in_=w_rows[:, k0 : k0 + channels])
+            for s in range(weight_loads[step]):
                 w_raw_of[step + s] = w_raw[:, s * STEP_CHANNELS : (s + 1) * STEP_CHANNELS]
 
         def transpose_weight(step):
@@ -131,66 +134,70 @@ def tile_dynamicrouting_k_kernel(tc, x, weight, bias, out):
             nc.vector.quantize_mx(out=w_codes[:].bitcast(FP8X4), scales=w_scales[:], in_=w_grouped_of[step][:])
             w_quantised_of[step] = (w_codes, w_scales)
 
-        def load_x(step):
-            if not exists(step):
-                return
-            k0 = step * STEP_CHANNELS
+        chunks = [(step * STEP_PASSES, STEP_PASSES) for step in range(STEPS - 1)]
+        chunks += [(PASSES - STEP_PASSES + c, 2) for c in range(0, STEP_PASSES, 2)]
+
+        def load_x(t):
+            c0, passes = chunks[t]
             x_raw = raw.tile([P, STEP_PASSES, PACK, PIXELS], BF16, bufs=12)
             nc.sync.dma_start(
-                out=x_raw[:],
-                in_=x_rows[k0 : k0 + STEP_CHANNELS, :].rearrange("(c p t) n -> p c t n", p=P, t=PACK),
+                out=x_raw[:, :passes],
+                in_=x_rows[c0 * K_PASS : (c0 + passes) * K_PASS, :].rearrange("(c p t) n -> p c t n", p=P, t=PACK),
             )
-            x_raw_of[step] = x_raw
+            x_raw_of[t] = x_raw
 
-        def regroup_x(step):
-            if not exists(step):
-                return
+        def regroup_x(t):
+            passes = chunks[t][1]
+            vector_passes = 3 if passes == STEP_PASSES and t % 8 in (1, 4, 6) else passes // 2
             x_grouped = stage.tile([P, STEP_PASSES, PIXELS, PACK], BF16, align_bytes=64)
-            x_from = x_raw_of[step][:].rearrange("p c t (m i) -> p c m t i", i=4)
+            x_from = x_raw_of[t][:].rearrange("p c t (m i) -> p c m t i", i=4)
             x_to = x_grouped[:].rearrange("p c (m i) t -> p c m t i", i=4)
-            nc.vector.tensor_copy(out=x_to[:, :VECTOR_PASSES], in_=x_from[:, :VECTOR_PASSES])
-            nc.scalar.copy(out=x_to[:, VECTOR_PASSES:], in_=x_from[:, VECTOR_PASSES:])
-            x_grouped_of[step] = x_grouped
+            paired = vector_passes - vector_passes % 2
+            if paired:
+                nc.vector.tensor_copy(out=x_to[:, :paired], in_=x_from[:, :paired])
+            if vector_passes % 2:
+                nc.vector.tensor_copy(out=x_to[:, paired], in_=x_from[:, paired])
+            nc.scalar.copy(out=x_to[:, vector_passes:passes], in_=x_from[:, vector_passes:passes])
+            x_grouped_of[t] = x_grouped
 
-        def quantise_x(step):
-            if not exists(step):
-                return
-            x_codes = stage.tile([P, STEP_PASSES * PIXELS], U32, align_bytes=64)
-            x_scales = stage.tile([P, STEP_PASSES * PIXELS], U8, align_bytes=64)
+        def quantise_x(t):
+            passes = chunks[t][1]
+            cols = slice(0, passes * PIXELS)
+            x_codes = stage.tile([P, STEP_PASSES * PIXELS], U32, align_bytes=64, bufs=6)
+            x_scales = stage.tile([P, STEP_PASSES * PIXELS], U8, align_bytes=64, bufs=6)
             nc.vector.quantize_mx(
-                out=x_codes[:].bitcast(FP8X4),
-                scales=x_scales[:],
-                in_=x_grouped_of[step][:].rearrange("p c n t -> p (c n t)"),
+                out=x_codes[:, cols].bitcast(FP8X4),
+                scales=x_scales[:, cols],
+                in_=x_grouped_of[t][:, :passes].rearrange("p c n t -> p (c n t)"),
             )
-            x_quantised_of[step] = (x_codes, x_scales)
+            x_quantised_of[t] = (x_codes, x_scales)
 
-        def multiply(step):
-            if not exists(step):
-                return
-            w_codes, w_scales = w_quantised_of[step]
-            x_codes, x_scales = x_quantised_of[step]
-            for c in range(STEP_PASSES):
-                g, c_in_group = divmod(step * STEP_PASSES + c, GROUP_PASSES)
+        def multiply(t):
+            c0, passes = chunks[t]
+            w_codes, w_scales = w_quantised_of[c0 // STEP_PASSES]
+            x_codes, x_scales = x_quantised_of[t]
+            for c in range(passes):
+                g, c_in_group = divmod(c0 + c, GROUP_PASSES)
                 if c_in_group == 0:
                     con_bank = sums.tile([P, BANK_WORDS], F32)
                     con_bank_of[g] = con_bank
-                cols = slice(c * P, (c + 1) * P)
+                x_cols = slice(c * PIXELS, (c + 1) * PIXELS)
+                w_pass = (c0 + c) % STEP_PASSES
+                w_cols = slice(w_pass * OUT_CHANNELS, (w_pass + 1) * OUT_CHANNELS)
                 nc.tensor.matmul_mx(
                     out=con_bank_of[g][:, :OUT_CHANNELS],
-                    lhsT=x_codes[:, cols].bitcast(FP8X4),
-                    lhsT_scale=x_scales[:, cols],
-                    rhs=w_codes[:, cols].bitcast(FP8X4),
-                    rhs_scale=w_scales[:, cols],
+                    lhsT=x_codes[:, x_cols].bitcast(FP8X4),
+                    lhsT_scale=x_scales[:, x_cols],
+                    rhs=w_codes[:, w_cols].bitcast(FP8X4),
+                    rhs_scale=w_scales[:, w_cols],
                     start=(c_in_group == 0),
                     stop=(c_in_group == GROUP_PASSES - 1),
                 )
 
-        def keep_warm(step, passes):
-            if not exists(step):
-                return
-            w_codes, w_scales = w_quantised_of[step]
-            x_codes, x_scales = x_quantised_of[step]
-            for _ in range(passes):
+        def keep_warm(t):
+            w_codes, w_scales = w_quantised_of[chunks[t][0] // STEP_PASSES]
+            x_codes, x_scales = x_quantised_of[t]
+            for _ in range(WARMING_PASSES):
                 nc.tensor.matmul_mx(
                     out=warm_bank[:],
                     lhsT=x_codes[:, :PIXELS].bitcast(FP8X4),
@@ -215,32 +222,40 @@ def tile_dynamicrouting_k_kernel(tc, x, weight, bias, out):
 
         dots_to_do = []
 
-        for t in range(-4, STEPS + 1):
-            load_weight(t + 4)
-            load_x(t)
-            regroup_x(t)
-            multiply(t - 1)
-            keep_warm(t - 1, TAIL_WARMING_PASSES if t == STEPS else WARMING_PASSES)
-            copy_weight_out(t + 3)
-            transpose_weight(t + 4)
-            quantise_weight(t + 2)
+        x_round = [t + X_FALLS_BACK * t // (len(chunks) - 1) for t in range(len(chunks))]
+        pass_round = [1 + max(x_round[t], chunks[t][0] // STEP_PASSES + 2) for t in range(len(chunks))]
+        group_round = [pass_round[t] for t in range(len(chunks)) if sum(chunks[t]) % GROUP_PASSES == 0]
+        for r in range(pass_round[-1] + 1):
+            new_chunks = [t for t in range(len(chunks)) if x_round[t] == r]
+            for t in new_chunks:
+                load_x(t)
+            load_weight(r)
+            for t in new_chunks:
+                regroup_x(t)
+            for t in range(len(chunks)):
+                if pass_round[t] == r:
+                    multiply(t)
+            copy_weight_out(r - 1)
+            transpose_weight(r)
+            quantise_weight(r - 2)
             for _ in range(min(ROUND_DOTS, len(dots_to_do))):
                 g, h = dots_to_do.pop(0)
                 dot(g, h)
-            quantise_x(t)
-            if t == 2:
+            for t in new_chunks:
+                quantise_x(t)
+            if r == 2:
                 nc.vector.tensor_copy(out=bias_square_f32[:], in_=bias_square[:])
-            group, step_in_group = divmod(t - TAKE_ROUND, GROUP_STEPS)
-            if step_in_group == 0 and 0 <= group < GROUPS - 1:
-                take_con(group)
-                dots_to_do.extend((group, h) for h in range(group))
-            group, step_in_group = divmod(t - MIRROR_ROUND, GROUP_STEPS)
-            if step_in_group == 0 and 0 < group < GROUPS - 2:
-                mirror(group)
+            for g in range(GROUPS - 1):
+                if r == group_round[g] + TAKE_LAG:
+                    take_con(g)
+                    dots_to_do.extend((g, h) for h in range(g))
+                if 0 < g < GROUPS - 2 and r == group_round[g] + MIRROR_LAG:
+                    mirror(g)
 
         last = GROUPS - 1
         mirror(last - 1)
         take_con(last)
+        keep_warm(len(chunks) - 1)
         early_sum = routing.tile([P, GROUPS], F32)
         nc.vector.tensor_reduce(out=early_sum[:, :last], in_=gram[:, :last, :last], axis=AXIS_X, op=ADD)
         for h in range(last):

@@ -100,7 +100,7 @@ def tile_dynamicrouting_k_kernel(tc, x, weight, bias, out):
                 return
             k0 = step * STEP_CHANNELS
             channels = weight_loads[step] * STEP_CHANNELS
-            w_raw = raw.tile([P, WEIGHT_LOAD_STEPS * STEP_CHANNELS], BF16)
+            w_raw = raw.tile([P, WEIGHT_LOAD_STEPS * STEP_CHANNELS], BF16, align_bytes=256)
             nc.sync.dma_start(out=w_raw[:, :channels], in_=w_rows[:, k0 : k0 + channels])
             for s in range(weight_loads[step]):
                 w_raw_of[step + s] = w_raw[:, s * STEP_CHANNELS : (s + 1) * STEP_CHANNELS]
@@ -139,7 +139,7 @@ def tile_dynamicrouting_k_kernel(tc, x, weight, bias, out):
 
         def load_x(t):
             c0, passes = chunks[t]
-            x_raw = raw.tile([P, STEP_PASSES, PACK, PIXELS], BF16, bufs=12)
+            x_raw = raw.tile([P, STEP_PASSES, PACK, PIXELS], BF16, bufs=12, align_bytes=256)
             nc.sync.dma_start(
                 out=x_raw[:, :passes],
                 in_=x_rows[c0 * K_PASS : (c0 + passes) * K_PASS, :].rearrange("(c p t) n -> p c t n", p=P, t=PACK),

@@ -32,8 +32,9 @@ STEP_CHANNELS = STEP_PASSES * K_PASS
 WEIGHT_LOAD_STEPS = 2
 BANK_PASSES = 2
 BANK_WORDS = 512
+VECTOR_RUNS = 22
 X_FALLS_BACK = 4
-WARMING_PASSES = 10
+WARMING_PASSES = 8
 TAKE_LAG = 1
 MIRROR_LAG = 5
 ROUND_DOTS = 3
@@ -55,7 +56,7 @@ def tile_dynamicrouting_k_kernel(tc, x, weight, bias, out):
         stage = ctx.enter_context(tc.tile_pool(name="stage", bufs=3))
         routing = ctx.enter_context(tc.tile_pool(name="routing", bufs=1))
         banks = ctx.enter_context(tc.psum_pool(name="banks", bufs=5))
-        warming = ctx.enter_context(tc.psum_pool(name="warming", bufs=1))
+        twin = ctx.enter_context(tc.psum_pool(name="twin", bufs=1))
         sums = ctx.enter_context(tc.psum_pool(name="sums", bufs=2))
 
         ctx.enter_context(tc.manual_schedule())
@@ -79,7 +80,7 @@ def tile_dynamicrouting_k_kernel(tc, x, weight, bias, out):
         vector_scratch = routing.tile([P, GROUPS, OUT_CHANNELS], F32)
         scalar_scratch = routing.tile([P, OUT_CHANNELS], F32)
         con_bank_of = {}
-        warm_bank = warming.tile([P, BANK_WORDS], F32)
+        twin_bank = twin.tile([P, BANK_WORDS], F32)
 
         w_raw_of = {}
         w_banks_of = {}
@@ -135,7 +136,7 @@ def tile_dynamicrouting_k_kernel(tc, x, weight, bias, out):
             w_quantised_of[step] = (w_codes, w_scales)
 
         chunks = [(step * STEP_PASSES, STEP_PASSES) for step in range(STEPS - 1)]
-        chunks += [(PASSES - STEP_PASSES + c, 2) for c in range(0, STEP_PASSES, 2)]
+        chunks += [(PASSES - 4, 2), (PASSES - 2, 1), (PASSES - 1, 1)]
 
         def load_x(t):
             c0, passes = chunks[t]
@@ -148,17 +149,21 @@ def tile_dynamicrouting_k_kernel(tc, x, weight, bias, out):
 
         def regroup_x(t):
             passes = chunks[t][1]
-            vector_passes = 3 if passes == STEP_PASSES and t % 8 in (1, 4, 6) else passes // 2
             x_grouped = stage.tile([P, STEP_PASSES, PIXELS, PACK], BF16, align_bytes=64)
             x_from = x_raw_of[t][:].rearrange("p c t (m i) -> p c m t i", i=4)
             x_to = x_grouped[:].rearrange("p c (m i) t -> p c m t i", i=4)
+            x_grouped_of[t] = x_grouped
+            if passes == 1:
+                nc.vector.tensor_copy(out=x_to[:, 0, :VECTOR_RUNS], in_=x_from[:, 0, :VECTOR_RUNS])
+                nc.scalar.copy(out=x_to[:, 0, VECTOR_RUNS:], in_=x_from[:, 0, VECTOR_RUNS:])
+                return
+            vector_passes = 3 if passes == STEP_PASSES and t % 2 == 1 else passes // 2
             paired = vector_passes - vector_passes % 2
             if paired:
                 nc.vector.tensor_copy(out=x_to[:, :paired], in_=x_from[:, :paired])
             if vector_passes % 2:
                 nc.vector.tensor_copy(out=x_to[:, paired], in_=x_from[:, paired])
             nc.scalar.copy(out=x_to[:, vector_passes:passes], in_=x_from[:, vector_passes:passes])
-            x_grouped_of[t] = x_grouped
 
         def quantise_x(t):
             passes = chunks[t][1]
@@ -184,19 +189,21 @@ def tile_dynamicrouting_k_kernel(tc, x, weight, bias, out):
                 x_cols = slice(c * PIXELS, (c + 1) * PIXELS)
                 w_pass = (c0 + c) % STEP_PASSES
                 w_cols = slice(w_pass * OUT_CHANNELS, (w_pass + 1) * OUT_CHANNELS)
-                nc.tensor.matmul_mx(
-                    out=con_bank_of[g][:, :OUT_CHANNELS],
-                    lhsT=x_codes[:, x_cols].bitcast(FP8X4),
-                    lhsT_scale=x_scales[:, x_cols],
-                    rhs=w_codes[:, w_cols].bitcast(FP8X4),
-                    rhs_scale=w_scales[:, w_cols],
-                    start=(c_in_group == 0),
-                    stop=(c_in_group == GROUP_PASSES - 1),
-                )
+                for con_bank in [con_bank_of[g]] + ([twin_bank] if g == GROUPS - 1 else []):
+                    nc.tensor.matmul_mx(
+                        out=con_bank[:, :OUT_CHANNELS],
+                        lhsT=x_codes[:, x_cols].bitcast(FP8X4),
+                        lhsT_scale=x_scales[:, x_cols],
+                        rhs=w_codes[:, w_cols].bitcast(FP8X4),
+                        rhs_scale=w_scales[:, w_cols],
+                        start=(c_in_group == 0),
+                        stop=(c_in_group == GROUP_PASSES - 1),
+                    )
 
         def keep_warm(t):
             w_codes, w_scales = w_quantised_of[chunks[t][0] // STEP_PASSES]
             x_codes, x_scales = x_quantised_of[t]
+            warm_bank = banks.tile([P, BANK_WORDS], F32, tag="bank")
             for _ in range(WARMING_PASSES):
                 nc.tensor.matmul_mx(
                     out=warm_bank[:],
@@ -208,13 +215,13 @@ def tile_dynamicrouting_k_kernel(tc, x, weight, bias, out):
                     stop=True,
                 )
 
-        def take_con(g):
-            nc.scalar.copy(out=con[:, g, :], in_=con_bank_of[g][:, :OUT_CHANNELS])
+        def take_con(g, con_bank):
+            nc.scalar.copy(out=con[:, g, :], in_=con_bank[:, :OUT_CHANNELS])
             nc.scalar.activation(out=scalar_scratch[:], in_=con[:, g, :], func=SQUARE, accum_out=gram[:, g, g : g + 1])
 
-        def dot(g, h):
+        def dot(con_of_g, g, h):
             nc.vector.scalar_tensor_tensor(
-                out=vector_scratch[:, h, :], in0=con[:, g, :], scalar=1.0, in1=con[:, h, :], op0=MULT, op1=MULT, accum_out=gram[:, g, h : h + 1]
+                out=vector_scratch[:, h, :], in0=con_of_g, scalar=1.0, in1=con[:, h, :], op0=MULT, op1=MULT, accum_out=gram[:, g, h : h + 1]
             )
 
         def mirror(g):
@@ -240,26 +247,26 @@ def tile_dynamicrouting_k_kernel(tc, x, weight, bias, out):
             quantise_weight(r - 2)
             for _ in range(min(ROUND_DOTS, len(dots_to_do))):
                 g, h = dots_to_do.pop(0)
-                dot(g, h)
+                dot(con[:, g, :], g, h)
             for t in new_chunks:
                 quantise_x(t)
             if r == 2:
                 nc.vector.tensor_copy(out=bias_square_f32[:], in_=bias_square[:])
             for g in range(GROUPS - 1):
                 if r == group_round[g] + TAKE_LAG:
-                    take_con(g)
+                    take_con(g, con_bank_of[g])
                     dots_to_do.extend((g, h) for h in range(g))
                 if 0 < g < GROUPS - 2 and r == group_round[g] + MIRROR_LAG:
                     mirror(g)
 
         last = GROUPS - 1
         mirror(last - 1)
-        take_con(last)
+        take_con(last, twin_bank)
         keep_warm(len(chunks) - 1)
         early_sum = routing.tile([P, GROUPS], F32)
         nc.vector.tensor_reduce(out=early_sum[:, :last], in_=gram[:, :last, :last], axis=AXIS_X, op=ADD)
         for h in range(last):
-            dot(last, h)
+            dot(con_bank_of[last][:, :OUT_CHANNELS], last, h)
         mirror(last)
 
         row_sum = routing.tile([P, GROUPS], F32)
@@ -301,6 +308,6 @@ def tile_dynamicrouting_k_kernel(tc, x, weight, bias, out):
             nc.tensor.matmul(out_bank[:, :PIXELS], lhsT=con[:, g, :], rhs=diagonals[:, d, :], start=False, stop=False)
         for e in range(2):
             nc.tensor.matmul(out_bank[:, :PIXELS], lhsT=even_odd[:, e, :], rhs=ident[:], start=False, stop=(e == 1))
-        result = routing.tile([P, PIXELS], F32)
+        result = routing.tile([P, PIXELS], F32, align_bytes=256)
         nc.vector.tensor_copy(out=result[:], in_=out_bank[:, :PIXELS])
         nc.sync.dma_start(out=out_rows, in_=result[:])

from contextlib import ExitStack

import concourse.mybir as mybir
from concourse.masks import make_identity

F32 = mybir.dt.float32
BF16 = mybir.dt.bfloat16
U32 = mybir.dt.uint32
U8 = mybir.dt.uint8
FP8X4 = mybir.dt.float8_e4m3fn_x4
ADD = mybir.AluOpType.add
MULT = mybir.AluOpType.mult
AXIS_X = mybir.AxisListType.X
SIGMOID = mybir.ActivationFunctionType.Sigmoid
SQUARE = mybir.ActivationFunctionType.Square
COPY = mybir.ActivationFunctionType.Copy

P = 128
PACK = 4
K_PASS = P * PACK
GROUPS = 8
GROUP_CHANNELS = 8192
OUT_CHANNELS = 128
PIXELS = 128
GROUP_PASSES = GROUP_CHANNELS // K_PASS
PASSES = GROUPS * GROUP_PASSES

STEP_PASSES = 4
STEPS = PASSES // STEP_PASSES
GROUP_STEPS = GROUP_PASSES // STEP_PASSES
STEP_CHANNELS = STEP_PASSES * K_PASS
WEIGHT_LOAD_STEPS = 2
BANK_PASSES = 2
BANK_WORDS = 512
VECTOR_RUNS = 22
X_FALLS_BACK = 4
WARMING_PASSES = 8
TAKE_LAG = 1
MIRROR_LAG = 5
ROUND_DOTS = 3
SUMMED_ON_VECTOR = 6

FLOPS = 2 * OUT_CHANNELS * GROUPS * GROUP_CHANNELS * PIXELS


def tile_dynamicrouting_k_kernel(tc, x, weight, bias, out):
    nc = tc.nc
    x_rows = x.rearrange("b c h w -> (b c) (h w)")
    w_rows = weight.rearrange("o c a b -> o (c a b)")
    bias_row = bias.rearrange("a o b c -> a (o b c)")
    out_rows = out.rearrange("b o h w -> (b o) (h w)")

    with ExitStack() as ctx:
        const = ctx.enter_context(tc.tile_pool(name="const", bufs=1))
        raw = ctx.enter_context(tc.tile_pool(name="raw", bufs=8))
        stage = ctx.enter_context(tc.tile_pool(name="stage", bufs=3))
        routing = ctx.enter_context(tc.tile_pool(name="routing", bufs=1))
        banks = ctx.enter_context(tc.psum_pool(name="banks", bufs=5))
        twin = ctx.enter_context(tc.psum_pool(name="twin", bufs=1))
        sums = ctx.enter_context(tc.psum_pool(name="sums", bufs=2))

        ctx.enter_context(tc.manual_schedule())

        ident = const.tile([P, P], F32)
        make_identity(nc, ident[:])

        warm = const.tile([P, 1], F32)
        nc.vector.memset(warm[:], 0.0)
        nc.scalar.activation(out=warm[:], in_=warm[:], func=SIGMOID)

        bias_square = const.tile([P, P], BF16)
        nc.vector.memset(bias_square[:], 0.0)
        nc.scalar.dma_start(out=bias_square[0:1, :], in_=bias_row)
        bias_square_f32 = const.tile([P, P], F32)
        ones = const.tile([P, P], F32)
        nc.vector.memset(ones[:], 1.0)

        con = routing.tile([P, GROUPS, OUT_CHANNELS], F32)
        gram = routing.tile([P, GROUPS, GROUPS], F32)
        vector_scratch = routing.tile([P, GROUPS, OUT_CHANNELS], F32)
        scalar_scratch = routing.tile([P, OUT_CHANNELS], F32)
        con_bank_of = {}
        twin_bank = twin.tile([P, BANK_WORDS], F32)

        w_raw_of = {}
        w_banks_of = {}
        w_grouped_of = {}
        w_quantised_of = {}
        x_raw_of = {}
        x_grouped_of = {}
        x_quantised_of = {}

        def exists(step):
            return 0 <= step < STEPS

        weight_loads = {0: 1, 1: 1}
        weight_loads.update({step: WEIGHT_LOAD_STEPS for step in range(2, STEPS, WEIGHT_LOAD_STEPS)})

        def load_weight(step):
            if step not in weight_loads:
                return
            k0 = step * STEP_CHANNELS
            channels = weight_loads[step] * STEP_CHANNELS
            w_raw = raw.tile([P, WEIGHT_LOAD_STEPS * STEP_CHANNELS], BF16, align_bytes=256)
            nc.sync.dma_start(out=w_raw[:, :channels], in_=w_rows[:, k0 : k0 + channels])
            for s in range(weight_loads[step]):
                w_raw_of[step + s] = w_raw[:, s * STEP_CHANNELS : (s + 1) * STEP_CHANNELS]

        def transpose_weight(step):
            if not exists(step):
                return
            w_words = w_raw_of[step].bitcast(F32).rearrange("o (c p u) -> o c u p", p=P, u=2)
            w_banks_of[step] = []
            for c0 in range(0, STEP_PASSES, BANK_PASSES):
                bank = banks.tile([P, BANK_PASSES, 2, OUT_CHANNELS], F32, tag="bank")
                for c in range(BANK_PASSES):
                    for u in range(2):
                        nc.tensor.transpose(bank[:, c, u, :], w_words[:, c0 + c, u, :], ident[:])
                w_banks_of[step].append(bank)

        def copy_weight_out(step):
            if not exists(step):
                return
            w_grouped = stage.tile([P, STEP_PASSES * OUT_CHANNELS * PACK], BF16, align_bytes=64)
            w_grouped_words = w_grouped[:].bitcast(F32).rearrange("p (b c o u) -> p b c o u", c=BANK_PASSES, o=OUT_CHANNELS, u=2)
            for b, bank in enumerate(w_banks_of[step]):
                nc.scalar.copy(out=w_grouped_words[:, b], in_=bank[:].rearrange("p c u o -> p c o u"))
            w_grouped_of[step] = w_grouped

        def quantise_weight(step):
            if not exists(step):
                return
            w_codes = stage.tile([P, STEP_PASSES * OUT_CHANNELS], U32, align_bytes=64, bufs=5)
            w_scales = stage.tile([P, STEP_PASSES * OUT_CHANNELS], U8, align_bytes=64, bufs=5)
            nc.vector.quantize_mx(out=w_codes[:].bitcast(FP8X4), scales=w_scales[:], in_=w_grouped_of[step][:])
            w_quantised_of[step] = (w_codes, w_scales)

        chunks = [(step * STEP_PASSES, STEP_PASSES) for step in range(STEPS - 1)]
        chunks += [(PASSES - 4, 2), (PASSES - 2, 1), (PASSES - 1, 1)]

        def load_x(t):
            c0, passes = chunks[t]
            x_raw = raw.tile([P, STEP_PASSES, PACK, PIXELS], BF16, bufs=12, align_bytes=256)
            nc.sync.dma_start(
                out=x_raw[:, :passes],
                in_=x_rows[c0 * K_PASS : (c0 + passes) * K_PASS, :].rearrange("(c p t) n -> p c t n", p=P, t=PACK),
            )
            x_raw_of[t] = x_raw

        def regroup_x(t):
            passes = chunks[t][1]
            x_grouped = stage.tile([P, STEP_PASSES, PIXELS, PACK], BF16, align_bytes=64)
            x_from = x_raw_of[t][:].rearrange("p c t (m i) -> p c m t i", i=4)
            x_to = x_grouped[:].rearrange("p c (m i) t -> p c m t i", i=4)
            x_grouped_of[t] = x_grouped
            if passes == 1:
                nc.vector.tensor_copy(out=x_to[:, 0, :VECTOR_RUNS], in_=x_from[:, 0, :VECTOR_RUNS])
                nc.scalar.copy(out=x_to[:, 0, VECTOR_RUNS:], in_=x_from[:, 0, VECTOR_RUNS:])
                return
            vector_passes = 3 if passes == STEP_PASSES and t % 2 == 1 else passes // 2
            paired = vector_passes - vector_passes % 2
            if paired:
                nc.vector.tensor_copy(out=x_to[:, :paired], in_=x_from[:, :paired])
            if vector_passes % 2:
                nc.vector.tensor_copy(out=x_to[:, paired], in_=x_from[:, paired])
            nc.scalar.copy(out=x_to[:, vector_passes:passes], in_=x_from[:, vector_passes:passes])

        def quantise_x(t):
            passes = chunks[t][1]
            cols = slice(0, passes * PIXELS)
            x_codes = stage.tile([P, STEP_PASSES * PIXELS], U32, align_bytes=64, bufs=6)
            x_scales = stage.tile([P, STEP_PASSES * PIXELS], U8, align_bytes=64, bufs=6)
            nc.vector.quantize_mx(
                out=x_codes[:, cols].bitcast(FP8X4),
                scales=x_scales[:, cols],
                in_=x_grouped_of[t][:, :passes].rearrange("p c n t -> p (c n t)"),
            )
            x_quantised_of[t] = (x_codes, x_scales)

        def multiply(t):
            c0, passes = chunks[t]
            w_codes, w_scales = w_quantised_of[c0 // STEP_PASSES]
            x_codes, x_scales = x_quantised_of[t]
            for c in range(passes):
                g, c_in_group = divmod(c0 + c, GROUP_PASSES)
                if c_in_group == 0:
                    con_bank = sums.tile([P, BANK_WORDS], F32)
                    con_bank_of[g] = con_bank
                x_cols = slice(c * PIXELS, (c + 1) * PIXELS)
                w_pass = (c0 + c) % STEP_PASSES
                w_cols = slice(w_pass * OUT_CHANNELS, (w_pass + 1) * OUT_CHANNELS)
                for con_bank in [con_bank_of[g]] + ([twin_bank] if g == GROUPS - 1 else []):
                    nc.tensor.matmul_mx(
                        out=con_bank[:, :OUT_CHANNELS],
                        lhsT=x_codes[:, x_cols].bitcast(FP8X4),
                        lhsT_scale=x_scales[:, x_cols],
                        rhs=w_codes[:, w_cols].bitcast(FP8X4),
                        rhs_scale=w_scales[:, w_cols],
                        start=(c_in_group == 0),
                        stop=(c_in_group == GROUP_PASSES - 1),
                    )

        def keep_warm(t):
            w_codes, w_scales = w_quantised_of[chunks[t][0] // STEP_PASSES]
            x_codes, x_scales = x_quantised_of[t]
            warm_bank = banks.tile([P, BANK_WORDS], F32, tag="bank")
            for _ in range(WARMING_PASSES):
                nc.tensor.matmul_mx(
                    out=warm_bank[:],
                    lhsT=x_codes[:, :PIXELS].bitcast(FP8X4),
                    lhsT_scale=x_scales[:, :PIXELS],
                    rhs=w_codes[:].bitcast(FP8X4),
                    rhs_scale=w_scales[:],
                    start=True,
                    stop=True,
                )

        def take_con(g, con_bank):
            nc.scalar.copy(out=con[:, g, :], in_=con_bank[:, :OUT_CHANNELS])
            nc.scalar.activation(out=scalar_scratch[:], in_=con[:, g, :], func=SQUARE, accum_out=gram[:, g, g : g + 1])

        def dot(con_of_g, g, h):
            nc.vector.scalar_tensor_tensor(
                out=vector_scratch[:, h, :], in0=con_of_g, scalar=1.0, in1=con[:, h, :], op0=MULT, op1=MULT, accum_out=gram[:, g, h : h + 1]
            )

        def mirror(g):
            nc.scalar.copy(out=gram[:, 0:g, g], in_=gram[:, g, 0:g])

        dots_to_do = []

        x_round = [t + X_FALLS_BACK * t // (len(chunks) - 1) for t in range(len(chunks))]
        pass_round = [1 + max(x_round[t], chunks[t][0] // STEP_PASSES + 2) for t in range(len(chunks))]
        group_round = [pass_round[t] for t in range(len(chunks)) if sum(chunks[t]) % GROUP_PASSES == 0]
        for r in range(pass_round[-1] + 1):
            new_chunks = [t for t in range(len(chunks)) if x_round[t] == r]
            for t in new_chunks:
                load_x(t)
            load_weight(r)
            for t in new_chunks:
                regroup_x(t)
            for t in range(len(chunks)):
                if pass_round[t] == r:
                    multiply(t)
            copy_weight_out(r - 1)
            transpose_weight(r)
            quantise_weight(r - 2)
            for _ in range(min(ROUND_DOTS, len(dots_to_do))):
                g, h = dots_to_do.pop(0)
                dot(con[:, g, :], g, h)
            for t in new_chunks:
                quantise_x(t)
            if r == 2:
                nc.vector.tensor_copy(out=bias_square_f32[:], in_=bias_square[:])
            for g in range(GROUPS - 1):
                if r == group_round[g] + TAKE_LAG:
                    take_con(g, con_bank_of[g])
                    dots_to_do.extend((g, h) for h in range(g))
                if 0 < g < GROUPS - 2 and r == group_round[g] + MIRROR_LAG:
                    mirror(g)

        last = GROUPS - 1
        mirror(last - 1)
        take_con(last, twin_bank)
        keep_warm(len(chunks) - 1)
        early_sum = routing.tile([P, GROUPS], F32)
        nc.vector.tensor_reduce(out=early_sum[:, :last], in_=gram[:, :last, :last], axis=AXIS_X, op=ADD)
        for h in range(last):
            dot(con_bank_of[last][:, :OUT_CHANNELS], last, h)
        mirror(last)

        row_sum = routing.tile([P, GROUPS], F32)
        nc.vector.tensor_tensor(out=row_sum[:, :last], in0=early_sum[:, :last], in1=gram[:, last, :last], op=ADD)
        nc.vector.tensor_reduce(out=row_sum[:, last:], in_=gram[:, last, :], axis=AXIS_X, op=ADD)
        alpha = routing.tile([P, GROUPS], F32)
        nc.scalar.activation(out=alpha[:], in_=row_sum[:], func=SIGMOID, scale=0.5)

        terms = routing.tile([P, GROUPS, GROUPS + 1], F32)
        nc.vector.tensor_scalar(out=terms[:, :, GROUPS], in0=row_sum[:], scalar1=0.5, scalar2=None, op0=MULT)
        nc.vector.tensor_tensor(
            out=terms[:, :, :GROUPS], in0=gram[:], in1=alpha[:].unsqueeze(1).to_broadcast([P, GROUPS, GROUPS]), op=MULT
        )
        beta = routing.tile([P, GROUPS], F32)
        nc.vector.tensor_reduce(out=beta[:], in_=terms[:], axis=AXIS_X, op=ADD)
        last_alpha = routing.tile([P, GROUPS], F32)
        nc.scalar.activation(out=last_alpha[:], in_=beta[:], func=SIGMOID)

        out_bank = banks.tile([P, BANK_WORDS], F32, tag="bank")
        nc.tensor.matmul(out_bank[:, :PIXELS], lhsT=bias_square_f32[:], rhs=ones[:], start=True, stop=False)
        even_odd = routing.tile([P, 2, OUT_CHANNELS], F32)
        for g in range(SUMMED_ON_VECTOR):
            if g < 2:
                nc.vector.tensor_scalar(
                    out=even_odd[:, g, :], in0=con[:, g, :], scalar1=last_alpha[:, g : g + 1], scalar2=None, op0=MULT
                )
            else:
                nc.vector.scalar_tensor_tensor(
                    out=even_odd[:, g % 2, :],
                    in0=con[:, g, :],
                    scalar=last_alpha[:, g : g + 1],
                    in1=even_odd[:, g % 2, :],
                    op0=MULT,
                    op1=ADD,
                )
        diagonals = routing.tile([P, GROUPS - SUMMED_ON_VECTOR, PIXELS], F32)
        for d, g in enumerate(range(SUMMED_ON_VECTOR, GROUPS)):
            nc.scalar.activation(out=diagonals[:, d, :], in_=ident[:], func=COPY, scale=last_alpha[:, g : g + 1])
            nc.tensor.matmul(out_bank[:, :PIXELS], lhsT=con[:, g, :], rhs=diagonals[:, d, :], start=False, stop=False)
        for e in range(2):
            nc.tensor.matmul(out_bank[:, :PIXELS], lhsT=even_odd[:, e, :], rhs=ident[:], start=False, stop=(e == 1))
        result = routing.tile([P, PIXELS], F32, align_bytes=256)
        nc.vector.tensor_copy(out=result[:], in_=out_bank[:, :PIXELS])
        nc.sync.dma_start(out=out_rows, in_=result[:])
